import numpy as np
import ml_dtypes


def mxq(x, axis, fmt="e4m3"):
    dtype, down = {"e4m3": (ml_dtypes.float8_e4m3fn, 7), "e5m2": (ml_dtypes.float8_e5m2, 14)}[fmt]
    v = np.moveaxis(np.asarray(x, np.float32).astype(ml_dtypes.bfloat16).astype(np.float64), axis, -1)
    blocks = v.reshape(v.shape[:-1] + (-1, 32))
    amax = np.abs(blocks).max(-1, keepdims=True)
    byte = np.maximum(np.where(amax > 0, np.frexp(amax)[1] - 1 + 127, 0) - down, 1)
    scale = np.exp2(byte - 127.0)
    codes = (blocks / scale).astype(np.float32).astype(dtype).astype(np.float64)
    return np.moveaxis((codes * scale).reshape(v.shape), -1, axis)


WIDE = False


def mx_kscale(k):
    if not WIDE:
        return np.ones(k)
    levels = np.array([20, -20, 10, -10, 0])
    a = np.random.permutation(np.resize(levels, k // 512 * 4)).reshape(k // 512, 4)
    idx = np.arange(k)
    return np.exp2(a[idx // 512, idx % 128 // 32])


BF16 = ml_dtypes.bfloat16


def bf(x):
    return np.asarray(x, np.float32).astype(BF16)


def f64(x):
    return np.asarray(x).astype(np.float64)


B, S, D, F, P, NQ = 2, 128, 1024, 512, 1024, 3
LN_EPS = 1e-5


def layernorm(v, g, b):
    m = v.mean(-1, keepdims=True)
    var = v.var(-1, keepdims=True)
    return (v - m) / np.sqrt(var + LN_EPS) * g + b


def setup_inputs():
    s = mx_kscale(F)[None, :, None]
    in0 = bf(np.random.standard_normal((NQ, F, P)))
    pt_w = bf(np.random.standard_normal((NQ, D, P)) / np.sqrt(P))
    pln_g = bf(1.0 + 0.1 * np.random.standard_normal((NQ, D)))
    pln_b = bf(0.1 * np.random.standard_normal((NQ, D)))
    proto_w = bf(np.random.standard_normal((NQ, F, D)) * 0.5)
    g = bf(np.random.standard_normal((NQ, F, D)) * np.exp2(np.random.randint(-12, 1, (NQ, F, 1))) / s)
    prc = f64(in0) @ f64(pt_w).transpose(0, 2, 1)
    mu = prc.mean(-1)
    rstd = 1.0 / np.sqrt(prc.var(-1) + LN_EPS)
    return {"in_proto": bf(f64(in0) * s), "pt_w": pt_w, "pln_g": pln_g, "pln_b": pln_b, "proto_w": proto_w,
            "prc": np.asarray(prc, np.float32), "mu": np.asarray(mu, np.float32),
            "rstd": np.asarray(rstd, np.float32), "grad_out": g}


def reference(in_proto, pt_w, pln_g, pln_b, proto_w, prc, mu, rstd, grad_out):
    r = f64(rstd)[:, :, None]
    xh = (f64(prc) - f64(mu)[:, :, None]) * r
    gh = f64(grad_out) * f64(pln_g)[:, None, :]
    dprc = r * (gh - gh.mean(-1, keepdims=True) - xh * (gh * xh).mean(-1, keepdims=True))
    return mxq(dprc, 1, "e5m2").transpose(0, 2, 1) @ mxq(f64(in_proto), 1, "e4m3")

@@ -1,0 +1,214 @@
+from contextlib import ExitStack
+
+import concourse.mybir as mybir
+
+F32 = mybir.dt.float32
+BF16 = mybir.dt.bfloat16
+U32 = mybir.dt.uint32
+U8 = mybir.dt.uint8
+E4M3_X4 = mybir.dt.float8_e4m3fn_x4
+E5M2_X4 = mybir.dt.float8_e5m2_x4
+MULT = mybir.AluOpType.mult
+ADD = mybir.AluOpType.add
+IDENTITY = mybir.ActivationFunctionType.Identity
+
+NQ = 3
+F = 512
+D = 1024
+W = 1024
+P = 128
+PACK = 4
+BANK = 512
+HALVES = 2
+RUN = 4
+OUT_BUFS = 6
+ACC_BANKS = 5
+
+FLOPS = 2 * NQ * D * W * F
+BYTES = NQ * (F * W * 2 + F * D * 2 + F * D * 4 + D * 2 + 2 * F * 4 + D * W * 4)
+
+
+def interleave_rows(copy, grouped, rows):
+    copy(
+        out=grouped.rearrange("p (c i) j -> p c j i", i=RUN),
+        in_=rows.rearrange("p j (c i) -> p c j i", i=RUN),
+    )
+
+
+def tile_moietransformerblock_pb_v_kernel(
+    tc, in_proto, pt_w, pln_g, pln_b, proto_w, prc, mu, rstd, grad_out, out
+):
+    nc = tc.nc
+    with ExitStack() as stack:
+        consts = stack.enter_context(tc.tile_pool(name="consts", bufs=1))
+        inputs = stack.enter_context(tc.tile_pool(name="inputs", bufs=NQ))
+        work = stack.enter_context(tc.tile_pool(name="work", bufs=2))
+        stats = stack.enter_context(tc.tile_pool(name="stats", bufs=2))
+        stores = stack.enter_context(tc.tile_pool(name="stores", bufs=OUT_BUFS))
+        gain_psum = stack.enter_context(tc.psum_pool(name="gain_psum", bufs=NQ))
+        acc_psum = stack.enter_context(tc.psum_pool(name="acc_psum", bufs=ACC_BANKS))
+
+        ones = consts.tile([P, P], BF16)
+        nc.vector.memset(ones[:], 1.0)
+        gain_rows = []
+        for n in range(NQ):
+            gain_row = consts.tile([P, D], BF16, name="gain_row%d" % n)
+            nc.vector.memset(gain_row[:], 0.0)
+            gain_rows.append(gain_row)
+
+        rstd_sb = consts.tile([P, NQ, PACK], F32)
+        nc.scalar.dma_start(out=rstd_sb[:], in_=rstd.rearrange("n (p j) -> p n j", j=PACK))
+        mu_sb = consts.tile([P, NQ, PACK], F32)
+        nc.scalar.dma_start(out=mu_sb[:], in_=mu.rearrange("n (p j) -> p n j", j=PACK))
+        for n in range(NQ):
+            nc.scalar.dma_start(out=gain_rows[n][0:1, :], in_=pln_g[n : n + 1, :])
+
+        grads, protos, centred = [], [], []
+        for n in range(NQ):
+            grad_sb = inputs.tile([P, PACK, D], BF16)
+            nc.sync.dma_start(out=grad_sb[:], in_=grad_out[n].rearrange("(p j) d -> p j d", j=PACK))
+            proto_sb = inputs.tile([P, PACK, W], BF16)
+            nc.sync.dma_start(out=proto_sb[:], in_=in_proto[n].rearrange("(p j) w -> p j w", j=PACK))
+            xc_sb = inputs.tile([P, PACK, D], F32)
+            prc_rows = prc[n].rearrange("(p j) d -> p j d", j=PACK)
+            nc.sync.dma_start(out=xc_sb[:, 0:2, :], in_=prc_rows[:, 0:2, :])
+            nc.sync.dma_start(out=xc_sb[:, 2:4, :], in_=prc_rows[:, 2:4, :])
+            grads.append(grad_sb)
+            protos.append(proto_sb)
+            centred.append(xc_sb)
+
+        gains = []
+        for n in range(NQ):
+            gain = gain_psum.tile([P, D], BF16)
+            for h in range(HALVES):
+                cols = slice(h * BANK, (h + 1) * BANK)
+                nc.tensor.matmul(
+                    out=gain[:, cols], lhsT=ones[:], rhs=gain_rows[n][:, cols], start=True, stop=True
+                )
+            gains.append(gain)
+
+        neg_mu = consts.tile([P, NQ, PACK], F32)
+        nc.vector.tensor_scalar(out=neg_mu[:], in0=mu_sb[:], scalar1=-1.0, scalar2=None, op0=MULT)
+        neg_a2 = consts.tile([P, NQ, PACK], F32)
+        nc.vector.scalar_tensor_tensor(
+            out=neg_a2[:], in0=rstd_sb[:], scalar=-1.0 / D, in1=rstd_sb[:], op0=MULT, op1=MULT
+        )
+
+        proto_groups = {}
+
+        def prepare(n):
+            proto_grouped = work.tile([P, W, PACK], BF16, align_bytes=64)
+            proto_groups[n] = proto_grouped
+            interleave_rows(nc.scalar.copy, proto_grouped[:, 0:BANK, :], protos[n][:, :, 0:BANK])
+            for j in range(PACK):
+                nc.scalar.activation(
+                    out=centred[n][:, j, :],
+                    in_=centred[n][:, j, :],
+                    func=IDENTITY,
+                    bias=neg_mu[:, n, j : j + 1],
+                    scale=1.0,
+                )
+
+        prepare(0)
+        for n in range(NQ):
+            xc_sb = centred[n]
+            proto_grouped = proto_groups[n]
+
+            gs = work.tile([P, PACK, D], F32)
+            sum_gs = stats.tile([P, PACK], F32)
+            for j in range(PACK):
+                nc.vector.scalar_tensor_tensor(
+                    out=gs[:, j, :],
+                    in0=grads[n][:, j, :],
+                    scalar=rstd_sb[:, n, j : j + 1],
+                    in1=gains[n][:],
+                    op0=MULT,
+                    op1=MULT,
+                    accum_out=sum_gs[:, j : j + 1],
+                )
+            interleave_rows(
+                nc.vector.tensor_copy, proto_grouped[:, BANK:W, :], protos[n][:, :, BANK:W]
+            )
+            shift = stats.tile([P, PACK], F32)
+            nc.vector.tensor_scalar(
+                out=shift[:], in0=sum_gs[:], scalar1=-1.0 / D, scalar2=None, op0=MULT
+            )
+
+            sum_gx = stats.tile([P, PACK], F32)
+            for j in range(PACK):
+                product = work.tile([P, D], F32)
+                nc.vector.scalar_tensor_tensor(
+                    out=product[:],
+                    in0=xc_sb[:, j, :],
+                    scalar=1.0,
+                    in1=gs[:, j, :],
+                    op0=MULT,
+                    op1=MULT,
+                    accum_out=sum_gx[:, j : j + 1],
+                )
+                nc.scalar.activation(
+                    out=gs[:, j, :],
+                    in_=gs[:, j, :],
+                    func=IDENTITY,
+                    bias=shift[:, j : j + 1],
+                    scale=1.0,
+                )
+
+            proto_codes = work.tile([P, W], U32, align_bytes=64)
+            proto_scales = work.tile([P, W], U8, align_bytes=64)
+            nc.vector.quantize_mx(
+                out=proto_codes[:].bitcast(E4M3_X4),
+                scales=proto_scales[:],
+                in_=proto_grouped[:].rearrange("p w j -> p (w j)"),
+            )
+            slope = stats.tile([P, PACK], F32)
+            nc.vector.tensor_tensor(out=slope[:], in0=sum_gx[:], in1=neg_a2[:, n, :], op=MULT)
+
+            if n + 1 < NQ:
+                prepare(n + 1)
+
+            dprc = work.tile([P, PACK, D], BF16, bufs=1)
+            for j in range(PACK):
+                nc.vector.scalar_tensor_tensor(
+                    out=dprc[:, j, :],
+                    in0=xc_sb[:, j, :],
+                    scalar=slope[:, j : j + 1],
+                    in1=gs[:, j, :],
+                    op0=MULT,
+                    op1=ADD,
+                )
+
+            dprc_grouped = work.tile([P, D, PACK], BF16, bufs=1, align_bytes=64)
+            dprc_codes = work.tile([P, D], U32, align_bytes=64)
+            dprc_scales = work.tile([P, D], U8, align_bytes=64)
+            for h in range(HALVES):
+                cols = slice(h * BANK, (h + 1) * BANK)
+                interleave_rows(nc.vector.tensor_copy, dprc_grouped[:, cols, :], dprc[:, :, cols])
+            for h in range(HALVES):
+                cols = slice(h * BANK, (h + 1) * BANK)
+                nc.vector.quantize_mx(
+                    out=dprc_codes[:, cols].bitcast(E5M2_X4),
+                    scales=dprc_scales[:, cols],
+                    in_=dprc_grouped[:, cols, :].rearrange("p d j -> p (d j)"),
+                )
+
+            for c in range(D // P):
+                rows = slice(c * P, (c + 1) * P)
+                out_sb = stores.tile([P, W], F32)
+                for h in range(HALVES):
+                    cols = slice(h * BANK, (h + 1) * BANK)
+                    acc = acc_psum.tile([P, BANK], F32)
+                    nc.tensor.matmul_mx(
+                        out=acc[:],
+                        lhsT=dprc_codes[:, rows].bitcast(E5M2_X4),
+                        lhsT_scale=dprc_scales[:, rows],
+                        rhs=proto_codes[:, cols].bitcast(E4M3_X4),
+                        rhs_scale=proto_scales[:, cols],
+                        start=True,
+                        stop=True,
+                    )
+                    if n == NQ - 1 and h == 1:
+                        nc.vector.tensor_copy(out=out_sb[:, cols], in_=acc[:])
+                    else:
+                        nc.scalar.copy(out=out_sb[:, cols], in_=acc[:])
+                nc.sync.dma_start(out=out[n, rows, :], in_=out_sb[:])

@@ -40,6 +40,7 @@ def tile_moietransformerblock_pb_v_kernel(
 ):
     nc = tc.nc
     with ExitStack() as stack:
+        stack.enter_context(tc.manual_schedule())
         consts = stack.enter_context(tc.tile_pool(name="consts", bufs=1))
         inputs = stack.enter_context(tc.tile_pool(name="inputs", bufs=NQ))
         work = stack.enter_context(tc.tile_pool(name="work", bufs=2))
@@ -48,27 +49,28 @@ def tile_moietransformerblock_pb_v_kernel(
         gain_psum = stack.enter_context(tc.psum_pool(name="gain_psum", bufs=NQ))
         acc_psum = stack.enter_context(tc.psum_pool(name="acc_psum", bufs=ACC_BANKS))
 
-        ones = consts.tile([P, P], BF16)
-        nc.vector.memset(ones[:], 1.0)
         gain_rows = []
         for n in range(NQ):
             gain_row = consts.tile([P, D], BF16, name="gain_row%d" % n)
             nc.vector.memset(gain_row[:], 0.0)
             gain_rows.append(gain_row)
+        ones = consts.tile([P, P], BF16)
+        nc.vector.memset(ones[:], 1.0)
 
         rstd_sb = consts.tile([P, NQ, PACK], F32)
         nc.scalar.dma_start(out=rstd_sb[:], in_=rstd.rearrange("n (p j) -> p n j", j=PACK))
         mu_sb = consts.tile([P, NQ, PACK], F32)
         nc.scalar.dma_start(out=mu_sb[:], in_=mu.rearrange("n (p j) -> p n j", j=PACK))
-        for n in range(NQ):
-            nc.scalar.dma_start(out=gain_rows[n][0:1, :], in_=pln_g[n : n + 1, :])
 
         grads, protos, centred = [], [], []
         for n in range(NQ):
-            grad_sb = inputs.tile([P, PACK, D], BF16)
-            nc.sync.dma_start(out=grad_sb[:], in_=grad_out[n].rearrange("(p j) d -> p j d", j=PACK))
             proto_sb = inputs.tile([P, PACK, W], BF16)
             nc.sync.dma_start(out=proto_sb[:], in_=in_proto[n].rearrange("(p j) w -> p j w", j=PACK))
+            if n == 0:
+                for m in range(NQ):
+                    nc.sync.dma_start(out=gain_rows[m][0:1, :], in_=pln_g[m : m + 1, :])
+            grad_sb = inputs.tile([P, PACK, D], BF16)
+            nc.sync.dma_start(out=grad_sb[:], in_=grad_out[n].rearrange("(p j) d -> p j d", j=PACK))
             xc_sb = inputs.tile([P, PACK, D], F32)
             prc_rows = prc[n].rearrange("(p j) d -> p j d", j=PACK)
             nc.sync.dma_start(out=xc_sb[:, 0:2, :], in_=prc_rows[:, 0:2, :])
@@ -113,6 +115,9 @@ def tile_moietransformerblock_pb_v_kernel(
         for n in range(NQ):
             xc_sb = centred[n]
             proto_grouped = proto_groups[n]
+            interleave_rows(
+                nc.vector.tensor_copy, proto_grouped[:, BANK:W, :], protos[n][:, :, BANK:W]
+            )
 
             gs = work.tile([P, PACK, D], F32)
             sum_gs = stats.tile([P, PACK], F32)
@@ -126,9 +131,6 @@ def tile_moietransformerblock_pb_v_kernel(
                     op1=MULT,
                     accum_out=sum_gs[:, j : j + 1],
                 )
-            interleave_rows(
-                nc.vector.tensor_copy, proto_grouped[:, BANK:W, :], protos[n][:, :, BANK:W]
-            )
             shift = stats.tile([P, PACK], F32)
             nc.vector.tensor_scalar(
                 out=shift[:], in0=sum_gs[:], scalar1=-1.0 / D, scalar2=None, op0=MULT

@@ -89,8 +89,6 @@ def tile_moietransformerblock_pb_v_kernel(
                 )
             gains.append(gain)
 
-        neg_mu = consts.tile([P, NQ, PACK], F32)
-        nc.vector.tensor_scalar(out=neg_mu[:], in0=mu_sb[:], scalar1=-1.0, scalar2=None, op0=MULT)
         neg_a2 = consts.tile([P, NQ, PACK], F32)
         nc.vector.scalar_tensor_tensor(
             out=neg_a2[:], in0=rstd_sb[:], scalar=-1.0 / D, in1=rstd_sb[:], op0=MULT, op1=MULT
@@ -101,23 +99,28 @@ def tile_moietransformerblock_pb_v_kernel(
         def prepare(n):
             proto_grouped = work.tile([P, W, PACK], BF16, align_bytes=64)
             proto_groups[n] = proto_grouped
-            interleave_rows(nc.scalar.copy, proto_grouped[:, 0:BANK, :], protos[n][:, :, 0:BANK])
-            for j in range(PACK):
-                nc.scalar.activation(
-                    out=centred[n][:, j, :],
-                    in_=centred[n][:, j, :],
-                    func=IDENTITY,
-                    bias=neg_mu[:, n, j : j + 1],
-                    scale=1.0,
-                )
+            for h in range(HALVES):
+                cols = slice(h * BANK, (h + 1) * BANK)
+                interleave_rows(nc.scalar.copy, proto_grouped[:, cols, :], protos[n][:, :, cols])
 
         prepare(0)
         for n in range(NQ):
             xc_sb = centred[n]
             proto_grouped = proto_groups[n]
-            interleave_rows(
-                nc.vector.tensor_copy, proto_grouped[:, BANK:W, :], protos[n][:, :, BANK:W]
+
+            neg_mu = stats.tile([P, PACK], F32)
+            nc.vector.tensor_scalar(
+                out=neg_mu[:], in0=mu_sb[:, n, :], scalar1=-1.0, scalar2=None, op0=MULT
             )
+            for j in range(PACK):
+                nc.gpsimd.tensor_scalar(
+                    out=xc_sb[:, j, :],
+                    in0=xc_sb[:, j, :],
+                    scalar1=neg_mu[:, j : j + 1],
+                    scalar2=1.0,
+                    op0=ADD,
+                    op1=MULT,
+                )
 
             gs = work.tile([P, PACK, D], F32)
             sum_gs = stats.tile([P, PACK], F32)

@@ -10,6 +10,7 @@ E4M3_X4 = mybir.dt.float8_e4m3fn_x4
 E5M2_X4 = mybir.dt.float8_e5m2_x4
 MULT = mybir.AluOpType.mult
 ADD = mybir.AluOpType.add
+SUBTRACT = mybir.AluOpType.subtract
 IDENTITY = mybir.ActivationFunctionType.Identity
 
 NQ = 3
@@ -21,6 +22,7 @@ PACK = 4
 BANK = 512
 HALVES = 2
 RUN = 4
+LAST = PACK - 1
 OUT_BUFS = 6
 ACC_BANKS = 5
 
@@ -28,11 +30,12 @@ FLOPS = 2 * NQ * D * W * F
 BYTES = NQ * (F * W * 2 + F * D * 2 + F * D * 4 + D * 2 + 2 * F * 4 + D * W * 4)
 
 
-def interleave_rows(copy, grouped, rows):
-    copy(
-        out=grouped.rearrange("p (c i) j -> p c j i", i=RUN),
-        in_=rows.rearrange("p j (c i) -> p c j i", i=RUN),
-    )
+def by_column(grouped):
+    return grouped.rearrange("p (c i) j -> p c j i", i=RUN)
+
+
+def by_row(rows):
+    return rows.rearrange("p j (c i) -> p c j i", i=RUN)
 
 
 def tile_moietransformerblock_pb_v_kernel(
@@ -61,20 +64,21 @@ def tile_moietransformerblock_pb_v_kernel(
         nc.scalar.dma_start(out=rstd_sb[:], in_=rstd.rearrange("n (p j) -> p n j", j=PACK))
         mu_sb = consts.tile([P, NQ, PACK], F32)
         nc.scalar.dma_start(out=mu_sb[:], in_=mu.rearrange("n (p j) -> p n j", j=PACK))
+        nc.sync.dma_start(out=gain_rows[0][0:1, :], in_=pln_g[0:1, :])
+        for n in range(1, NQ):
+            nc.scalar.dma_start(out=gain_rows[n][0:1, :], in_=pln_g[n : n + 1, :])
 
         grads, protos, centred = [], [], []
         for n in range(NQ):
+            grad_sb = inputs.tile([P, PACK, D], BF16)
+            xc_sb = inputs.tile([P, PACK, D], F32)
+            grad_rows = grad_out[n].rearrange("(p j) d -> p j d", j=PACK)
+            prc_rows = prc[n].rearrange("(p j) d -> p j d", j=PACK)
+            for pair in (slice(0, 2), slice(2, 4)):
+                nc.sync.dma_start(out=grad_sb[:, pair, :], in_=grad_rows[:, pair, :])
+                nc.sync.dma_start(out=xc_sb[:, pair, :], in_=prc_rows[:, pair, :])
             proto_sb = inputs.tile([P, PACK, W], BF16)
             nc.sync.dma_start(out=proto_sb[:], in_=in_proto[n].rearrange("(p j) w -> p j w", j=PACK))
-            if n == 0:
-                for m in range(NQ):
-                    nc.sync.dma_start(out=gain_rows[m][0:1, :], in_=pln_g[m : m + 1, :])
-            grad_sb = inputs.tile([P, PACK, D], BF16)
-            nc.sync.dma_start(out=grad_sb[:], in_=grad_out[n].rearrange("(p j) d -> p j d", j=PACK))
-            xc_sb = inputs.tile([P, PACK, D], F32)
-            prc_rows = prc[n].rearrange("(p j) d -> p j d", j=PACK)
-            nc.sync.dma_start(out=xc_sb[:, 0:2, :], in_=prc_rows[:, 0:2, :])
-            nc.sync.dma_start(out=xc_sb[:, 2:4, :], in_=prc_rows[:, 2:4, :])
             grads.append(grad_sb)
             protos.append(proto_sb)
             centred.append(xc_sb)
@@ -89,115 +93,26 @@ def tile_moietransformerblock_pb_v_kernel(
                 )
             gains.append(gain)
 
-        neg_a2 = consts.tile([P, NQ, PACK], F32)
+        a2_over_d = consts.tile([P, NQ, PACK], F32)
         nc.vector.scalar_tensor_tensor(
-            out=neg_a2[:], in0=rstd_sb[:], scalar=-1.0 / D, in1=rstd_sb[:], op0=MULT, op1=MULT
+            out=a2_over_d[:], in0=rstd_sb[:], scalar=1.0 / D, in1=rstd_sb[:], op0=MULT, op1=MULT
         )
 
         proto_groups = {}
+        operands = {}
 
-        def prepare(n):
+        def regroup_proto(n):
             proto_grouped = work.tile([P, W, PACK], BF16, align_bytes=64)
             proto_groups[n] = proto_grouped
             for h in range(HALVES):
                 cols = slice(h * BANK, (h + 1) * BANK)
-                interleave_rows(nc.scalar.copy, proto_grouped[:, cols, :], protos[n][:, :, cols])
-
-        prepare(0)
-        for n in range(NQ):
-            xc_sb = centred[n]
-            proto_grouped = proto_groups[n]
-
-            neg_mu = stats.tile([P, PACK], F32)
-            nc.vector.tensor_scalar(
-                out=neg_mu[:], in0=mu_sb[:, n, :], scalar1=-1.0, scalar2=None, op0=MULT
-            )
-            for j in range(PACK):
-                nc.gpsimd.tensor_scalar(
-                    out=xc_sb[:, j, :],
-                    in0=xc_sb[:, j, :],
-                    scalar1=neg_mu[:, j : j + 1],
-                    scalar2=1.0,
-                    op0=ADD,
-                    op1=MULT,
+                nc.scalar.copy(
+                    out=by_column(proto_grouped[:, cols, :]), in_=by_row(protos[n][:, :, cols])
                 )
 
-            gs = work.tile([P, PACK, D], F32)
-            sum_gs = stats.tile([P, PACK], F32)
-            for j in range(PACK):
-                nc.vector.scalar_tensor_tensor(
-                    out=gs[:, j, :],
-                    in0=grads[n][:, j, :],
-                    scalar=rstd_sb[:, n, j : j + 1],
-                    in1=gains[n][:],
-                    op0=MULT,
-                    op1=MULT,
-                    accum_out=sum_gs[:, j : j + 1],
-                )
-            shift = stats.tile([P, PACK], F32)
-            nc.vector.tensor_scalar(
-                out=shift[:], in0=sum_gs[:], scalar1=-1.0 / D, scalar2=None, op0=MULT
-            )
-
-            sum_gx = stats.tile([P, PACK], F32)
-            for j in range(PACK):
-                product = work.tile([P, D], F32)
-                nc.vector.scalar_tensor_tensor(
-                    out=product[:],
-                    in0=xc_sb[:, j, :],
-                    scalar=1.0,
-                    in1=gs[:, j, :],
-                    op0=MULT,
-                    op1=MULT,
-                    accum_out=sum_gx[:, j : j + 1],
-                )
-                nc.scalar.activation(
-                    out=gs[:, j, :],
-                    in_=gs[:, j, :],
-                    func=IDENTITY,
-                    bias=shift[:, j : j + 1],
-                    scale=1.0,
-                )
-
-            proto_codes = work.tile([P, W], U32, align_bytes=64)
-            proto_scales = work.tile([P, W], U8, align_bytes=64)
-            nc.vector.quantize_mx(
-                out=proto_codes[:].bitcast(E4M3_X4),
-                scales=proto_scales[:],
-                in_=proto_grouped[:].rearrange("p w j -> p (w j)"),
-            )
-            slope = stats.tile([P, PACK], F32)
-            nc.vector.tensor_tensor(out=slope[:], in0=sum_gx[:], in1=neg_a2[:, n, :], op=MULT)
-
-            if n + 1 < NQ:
-                prepare(n + 1)
-
-            dprc = work.tile([P, PACK, D], BF16, bufs=1)
-            for j in range(PACK):
-                nc.vector.scalar_tensor_tensor(
-                    out=dprc[:, j, :],
-                    in0=xc_sb[:, j, :],
-                    scalar=slope[:, j : j + 1],
-                    in1=gs[:, j, :],
-                    op0=MULT,
-                    op1=ADD,
-                )
-
-            dprc_grouped = work.tile([P, D, PACK], BF16, bufs=1, align_bytes=64)
-            dprc_codes = work.tile([P, D], U32, align_bytes=64)
-            dprc_scales = work.tile([P, D], U8, align_bytes=64)
-            for h in range(HALVES):
-                cols = slice(h * BANK, (h + 1) * BANK)
-                interleave_rows(nc.vector.tensor_copy, dprc_grouped[:, cols, :], dprc[:, :, cols])
-            for h in range(HALVES):
-                cols = slice(h * BANK, (h + 1) * BANK)
-                nc.vector.quantize_mx(
-                    out=dprc_codes[:, cols].bitcast(E5M2_X4),
-                    scales=dprc_scales[:, cols],
-                    in_=dprc_grouped[:, cols, :].rearrange("p d j -> p (d j)"),
-                )
-
-            for c in range(D // P):
+        def multiply(n, half):
+            dprc_codes, dprc_scales, proto_codes, proto_scales = operands[n]
+            for c in range(half * BANK // P, (half + 1) * BANK // P):
                 rows = slice(c * P, (c + 1) * P)
                 out_sb = stores.tile([P, W], F32)
                 for h in range(HALVES):
@@ -212,8 +127,114 @@ def tile_moietransformerblock_pb_v_kernel(
                         start=True,
                         stop=True,
                     )
-                    if n == NQ - 1 and h == 1:
+                    if n == NQ - 1 and half == 1 and h == 1:
                         nc.vector.tensor_copy(out=out_sb[:, cols], in_=acc[:])
                     else:
                         nc.scalar.copy(out=out_sb[:, cols], in_=acc[:])
                 nc.sync.dma_start(out=out[n, rows, :], in_=out_sb[:])
+
+        for n in range(NQ):
+            xc_sb = centred[n]
+
+            neg_mu = stats.tile([P, PACK], F32)
+            nc.vector.tensor_scalar(
+                out=neg_mu[:], in0=mu_sb[:, n, :], scalar1=-1.0, scalar2=None, op0=MULT
+            )
+            for j in range(LAST):
+                nc.gpsimd.tensor_scalar(
+                    out=xc_sb[:, j, :],
+                    in0=xc_sb[:, j, :],
+                    scalar1=neg_mu[:, j : j + 1],
+                    scalar2=1.0,
+                    op0=ADD,
+                    op1=MULT,
+                )
+            nc.scalar.activation(
+                out=xc_sb[:, LAST, :],
+                in_=xc_sb[:, LAST, :],
+                func=IDENTITY,
+                bias=neg_mu[:, LAST : LAST + 1],
+                scale=1.0,
+            )
+
+            gs = work.tile([P, PACK, D], F32)
+            sum_gs = stats.tile([P, PACK], F32)
+            for j in range(PACK):
+                nc.vector.scalar_tensor_tensor(
+                    out=gs[:, j, :],
+                    in0=grads[n][:, j, :],
+                    scalar=rstd_sb[:, n, j : j + 1],
+                    in1=gains[n][:],
+                    op0=MULT,
+                    op1=MULT,
+                    accum_out=sum_gs[:, j : j + 1],
+                )
+            mean_gs = stats.tile([P, PACK], F32)
+            nc.vector.tensor_scalar(
+                out=mean_gs[:], in0=sum_gs[:], scalar1=1.0 / D, scalar2=None, op0=MULT
+            )
+
+            slope = stats.tile([P, PACK], F32)
+            for j in range(PACK):
+                product = work.tile([P, D], F32)
+                nc.vector.scalar_tensor_tensor(
+                    out=product[:],
+                    in0=xc_sb[:, j, :],
+                    scalar=a2_over_d[:, n, j : j + 1],
+                    in1=gs[:, j, :],
+                    op0=MULT,
+                    op1=MULT,
+                    accum_out=slope[:, j : j + 1],
+                )
+                if j < LAST:
+                    nc.scalar.activation(
+                        out=xc_sb[:, j, :],
+                        in_=xc_sb[:, j, :],
+                        func=IDENTITY,
+                        bias=mean_gs[:, j : j + 1],
+                        scale=slope[:, j : j + 1],
+                    )
+                else:
+                    nc.vector.tensor_scalar(
+                        out=xc_sb[:, j, :],
+                        in0=xc_sb[:, j, :],
+                        scalar1=slope[:, j : j + 1],
+                        scalar2=mean_gs[:, j : j + 1],
+                        op0=MULT,
+                        op1=ADD,
+                    )
+
+            if n > 0:
+                multiply(n - 1, 1)
+            if n == 0:
+                regroup_proto(0)
+            if n + 1 < NQ:
+                regroup_proto(n + 1)
+
+            dprc_codes = work.tile([P, D], U32, align_bytes=64)
+            dprc_scales = work.tile([P, D], U8, align_bytes=64)
+            proto_codes = work.tile([P, W], U32, align_bytes=64)
+            proto_scales = work.tile([P, W], U8, align_bytes=64)
+            operands[n] = (dprc_codes, dprc_scales, proto_codes, proto_scales)
+            for h in range(HALVES):
+                cols = slice(h * BANK, (h + 1) * BANK)
+                dprc_grouped = work.tile([P, BANK, PACK], BF16, align_bytes=64)
+                nc.vector.tensor_tensor(
+                    out=by_column(dprc_grouped[:]),
+                    in0=by_row(gs[:, :, cols]),
+                    in1=by_row(xc_sb[:, :, cols]),
+                    op=SUBTRACT,
+                )
+                if h == 0:
+                    nc.vector.quantize_mx(
+                        out=proto_codes[:].bitcast(E4M3_X4),
+                        scales=proto_scales[:],
+                        in_=proto_groups[n][:].rearrange("p w j -> p (w j)"),
+                    )
+                nc.vector.quantize_mx(
+                    out=dprc_codes[:, cols].bitcast(E5M2_X4),
+                    scales=dprc_scales[:, cols],
+                    in_=dprc_grouped[:].rearrange("p d j -> p (d j)"),
+                )
+            multiply(n, 0)
+        multiply(NQ - 1, 1)

@@ -21,6 +21,9 @@ P = 128
 PACK = 4
 BANK = 512
 HALVES = 2
+PIECES = 4
+TILES = D // P
+EARLY_TILES = 5
 RUN = 4
 LAST = PACK - 1
 OUT_BUFS = 6
@@ -69,6 +72,12 @@ def tile_moietransformerblock_pb_v_kernel(
             nc.scalar.dma_start(out=gain_rows[n][0:1, :], in_=pln_g[n : n + 1, :])
 
         grads, protos, centred = [], [], []
+
+        def load_proto(n):
+            proto_sb = inputs.tile([P, PACK, W], BF16)
+            nc.sync.dma_start(out=proto_sb[:], in_=in_proto[n].rearrange("(p j) w -> p j w", j=PACK))
+            protos.append(proto_sb)
+
         for n in range(NQ):
             grad_sb = inputs.tile([P, PACK, D], BF16)
             xc_sb = inputs.tile([P, PACK, D], F32)
@@ -77,11 +86,12 @@ def tile_moietransformerblock_pb_v_kernel(
             for pair in (slice(0, 2), slice(2, 4)):
                 nc.sync.dma_start(out=grad_sb[:, pair, :], in_=grad_rows[:, pair, :])
                 nc.sync.dma_start(out=xc_sb[:, pair, :], in_=prc_rows[:, pair, :])
-            proto_sb = inputs.tile([P, PACK, W], BF16)
-            nc.sync.dma_start(out=proto_sb[:], in_=in_proto[n].rearrange("(p j) w -> p j w", j=PACK))
             grads.append(grad_sb)
-            protos.append(proto_sb)
             centred.append(xc_sb)
+            if n == 0:
+                load_proto(0)
+            if n + 1 < NQ:
+                load_proto(n + 1)
 
         gains = []
         for n in range(NQ):
@@ -101,18 +111,18 @@ def tile_moietransformerblock_pb_v_kernel(
         proto_groups = {}
         operands = {}
 
-        def regroup_proto(n):
+        def regroup_proto(n, copies):
             proto_grouped = work.tile([P, W, PACK], BF16, align_bytes=64)
             proto_groups[n] = proto_grouped
             for h in range(HALVES):
                 cols = slice(h * BANK, (h + 1) * BANK)
-                nc.scalar.copy(
+                copies[h](
                     out=by_column(proto_grouped[:, cols, :]), in_=by_row(protos[n][:, :, cols])
                 )
 
-        def multiply(n, half):
+        def multiply(n, tiles):
             dprc_codes, dprc_scales, proto_codes, proto_scales = operands[n]
-            for c in range(half * BANK // P, (half + 1) * BANK // P):
+            for c in tiles:
                 rows = slice(c * P, (c + 1) * P)
                 out_sb = stores.tile([P, W], F32)
                 for h in range(HALVES):
@@ -127,10 +137,7 @@ def tile_moietransformerblock_pb_v_kernel(
                         start=True,
                         stop=True,
                     )
-                    if n == NQ - 1 and half == 1 and h == 1:
-                        nc.vector.tensor_copy(out=out_sb[:, cols], in_=acc[:])
-                    else:
-                        nc.scalar.copy(out=out_sb[:, cols], in_=acc[:])
+                    nc.scalar.copy(out=out_sb[:, cols], in_=acc[:])
                 nc.sync.dma_start(out=out[n, rows, :], in_=out_sb[:])
 
         for n in range(NQ):
@@ -205,36 +212,49 @@ def tile_moietransformerblock_pb_v_kernel(
                     )
 
             if n > 0:
-                multiply(n - 1, 1)
+                multiply(n - 1, range(EARLY_TILES, TILES))
             if n == 0:
-                regroup_proto(0)
+                regroup_proto(0, (nc.scalar.copy, nc.vector.tensor_copy))
             if n + 1 < NQ:
-                regroup_proto(n + 1)
+                regroup_proto(n + 1, (nc.scalar.copy, nc.scalar.copy))
 
             dprc_codes = work.tile([P, D], U32, align_bytes=64)
             dprc_scales = work.tile([P, D], U8, align_bytes=64)
             proto_codes = work.tile([P, W], U32, align_bytes=64)
             proto_scales = work.tile([P, W], U8, align_bytes=64)
             operands[n] = (dprc_codes, dprc_scales, proto_codes, proto_scales)
-            for h in range(HALVES):
-                cols = slice(h * BANK, (h + 1) * BANK)
-                dprc_grouped = work.tile([P, BANK, PACK], BF16, align_bytes=64)
+            pieces = {}
+
+            def subtract(piece):
+                cols = slice(piece * D // PIECES, (piece + 1) * D // PIECES)
+                dprc_grouped = work.tile([P, D // PIECES, PACK], BF16, bufs=3, align_bytes=64)
+                pieces[piece] = dprc_grouped
                 nc.vector.tensor_tensor(
                     out=by_column(dprc_grouped[:]),
                     in0=by_row(gs[:, :, cols]),
                     in1=by_row(xc_sb[:, :, cols]),
                     op=SUBTRACT,
                 )
-                if h == 0:
-                    nc.vector.quantize_mx(
-                        out=proto_codes[:].bitcast(E4M3_X4),
-                        scales=proto_scales[:],
-                        in_=proto_groups[n][:].rearrange("p w j -> p (w j)"),
-                    )
+
+            def quantise(piece):
+                cols = slice(piece * D // PIECES, (piece + 1) * D // PIECES)
                 nc.vector.quantize_mx(
                     out=dprc_codes[:, cols].bitcast(E5M2_X4),
                     scales=dprc_scales[:, cols],
-                    in_=dprc_grouped[:].rearrange("p d j -> p (d j)"),
+                    in_=pieces[piece][:].rearrange("p d j -> p (d j)"),
                 )
-            multiply(n, 0)
-        multiply(NQ - 1, 1)
+
+            subtract(0)
+            nc.vector.quantize_mx(
+                out=proto_codes[:].bitcast(E4M3_X4),
+                scales=proto_scales[:],
+                in_=proto_groups[n][:].rearrange("p w j -> p (w j)"),
+            )
+            quantise(0)
+            subtract(1)
+            for piece in range(2, PIECES):
+                subtract(piece)
+                quantise(piece - 1)
+            quantise(PIECES - 1)
+            multiply(n, range(EARLY_TILES))
+        multiply(NQ - 1, range(EARLY_TILES, TILES))

@@ -46,7 +46,6 @@ def tile_moietransformerblock_pb_v_kernel(
 ):
     nc = tc.nc
     with ExitStack() as stack:
-        stack.enter_context(tc.manual_schedule())
         consts = stack.enter_context(tc.tile_pool(name="consts", bufs=1))
         inputs = stack.enter_context(tc.tile_pool(name="inputs", bufs=NQ))
         work = stack.enter_context(tc.tile_pool(name="work", bufs=2))

from contextlib import ExitStack

import concourse.mybir as mybir

F32 = mybir.dt.float32
BF16 = mybir.dt.bfloat16
U32 = mybir.dt.uint32
U8 = mybir.dt.uint8
E4M3_X4 = mybir.dt.float8_e4m3fn_x4
E5M2_X4 = mybir.dt.float8_e5m2_x4
MULT = mybir.AluOpType.mult
ADD = mybir.AluOpType.add
SUBTRACT = mybir.AluOpType.subtract
IDENTITY = mybir.ActivationFunctionType.Identity

NQ = 3
F = 512
D = 1024
W = 1024
P = 128
PACK = 4
BANK = 512
HALVES = 2
PIECES = 4
TILES = D // P
EARLY_TILES = 5
RUN = 4
LAST = PACK - 1
OUT_BUFS = 6
ACC_BANKS = 5

FLOPS = 2 * NQ * D * W * F
BYTES = NQ * (F * W * 2 + F * D * 2 + F * D * 4 + D * 2 + 2 * F * 4 + D * W * 4)


def by_column(grouped):
    return grouped.rearrange("p (c i) j -> p c j i", i=RUN)


def by_row(rows):
    return rows.rearrange("p j (c i) -> p c j i", i=RUN)


def tile_moietransformerblock_pb_v_kernel(
    tc, in_proto, pt_w, pln_g, pln_b, proto_w, prc, mu, rstd, grad_out, out
):
    nc = tc.nc
    with ExitStack() as stack:
        consts = stack.enter_context(tc.tile_pool(name="consts", bufs=1))
        inputs = stack.enter_context(tc.tile_pool(name="inputs", bufs=NQ))
        work = stack.enter_context(tc.tile_pool(name="work", bufs=2))
        stats = stack.enter_context(tc.tile_pool(name="stats", bufs=2))
        stores = stack.enter_context(tc.tile_pool(name="stores", bufs=OUT_BUFS))
        gain_psum = stack.enter_context(tc.psum_pool(name="gain_psum", bufs=NQ))
        acc_psum = stack.enter_context(tc.psum_pool(name="acc_psum", bufs=ACC_BANKS))

        gain_rows = []
        for n in range(NQ):
            gain_row = consts.tile([P, D], BF16, name="gain_row%d" % n)
            nc.vector.memset(gain_row[:], 0.0)
            gain_rows.append(gain_row)
        ones = consts.tile([P, P], BF16)
        nc.vector.memset(ones[:], 1.0)

        rstd_sb = consts.tile([P, NQ, PACK], F32)
        nc.scalar.dma_start(out=rstd_sb[:], in_=rstd.rearrange("n (p j) -> p n j", j=PACK))
        mu_sb = consts.tile([P, NQ, PACK], F32)
        nc.scalar.dma_start(out=mu_sb[:], in_=mu.rearrange("n (p j) -> p n j", j=PACK))
        nc.sync.dma_start(out=gain_rows[0][0:1, :], in_=pln_g[0:1, :])
        for n in range(1, NQ):
            nc.scalar.dma_start(out=gain_rows[n][0:1, :], in_=pln_g[n : n + 1, :])

        grads, protos, centred = [], [], []

        def load_proto(n):
            proto_sb = inputs.tile([P, PACK, W], BF16)
            nc.sync.dma_start(out=proto_sb[:], in_=in_proto[n].rearrange("(p j) w -> p j w", j=PACK))
            protos.append(proto_sb)

        for n in range(NQ):
            grad_sb = inputs.tile([P, PACK, D], BF16)
            xc_sb = inputs.tile([P, PACK, D], F32)
            grad_rows = grad_out[n].rearrange("(p j) d -> p j d", j=PACK)
            prc_rows = prc[n].rearrange("(p j) d -> p j d", j=PACK)
            for pair in (slice(0, 2), slice(2, 4)):
                nc.sync.dma_start(out=grad_sb[:, pair, :], in_=grad_rows[:, pair, :])
                nc.sync.dma_start(out=xc_sb[:, pair, :], in_=prc_rows[:, pair, :])
            grads.append(grad_sb)
            centred.append(xc_sb)
            if n == 0:
                load_proto(0)
            if n + 1 < NQ:
                load_proto(n + 1)

        gains = []
        for n in range(NQ):
            gain = gain_psum.tile([P, D], BF16)
            for h in range(HALVES):
                cols = slice(h * BANK, (h + 1) * BANK)
                nc.tensor.matmul(
                    out=gain[:, cols], lhsT=ones[:], rhs=gain_rows[n][:, cols], start=True, stop=True
                )
            gains.append(gain)

        a2_over_d = consts.tile([P, NQ, PACK], F32)
        nc.vector.scalar_tensor_tensor(
            out=a2_over_d[:], in0=rstd_sb[:], scalar=1.0 / D, in1=rstd_sb[:], op0=MULT, op1=MULT
        )

        proto_groups = {}
        operands = {}

        def regroup_proto(n, copies):
            proto_grouped = work.tile([P, W, PACK], BF16, align_bytes=64)
            proto_groups[n] = proto_grouped
            for h in range(HALVES):
                cols = slice(h * BANK, (h + 1) * BANK)
                copies[h](
                    out=by_column(proto_grouped[:, cols, :]), in_=by_row(protos[n][:, :, cols])
                )

        def multiply(n, tiles):
            dprc_codes, dprc_scales, proto_codes, proto_scales = operands[n]
            for c in tiles:
                rows = slice(c * P, (c + 1) * P)
                out_sb = stores.tile([P, W], F32)
                for h in range(HALVES):
                    cols = slice(h * BANK, (h + 1) * BANK)
                    acc = acc_psum.tile([P, BANK], F32)
                    nc.tensor.matmul_mx(
                        out=acc[:],
                        lhsT=dprc_codes[:, rows].bitcast(E5M2_X4),
                        lhsT_scale=dprc_scales[:, rows],
                        rhs=proto_codes[:, cols].bitcast(E4M3_X4),
                        rhs_scale=proto_scales[:, cols],
                        start=True,
                        stop=True,
                    )
                    nc.scalar.copy(out=out_sb[:, cols], in_=acc[:])
                nc.sync.dma_start(out=out[n, rows, :], in_=out_sb[:])

        for n in range(NQ):
            xc_sb = centred[n]

            neg_mu = stats.tile([P, PACK], F32)
            nc.vector.tensor_scalar(
                out=neg_mu[:], in0=mu_sb[:, n, :], scalar1=-1.0, scalar2=None, op0=MULT
            )
            for j in range(LAST):
                nc.gpsimd.tensor_scalar(
                    out=xc_sb[:, j, :],
                    in0=xc_sb[:, j, :],
                    scalar1=neg_mu[:, j : j + 1],
                    scalar2=1.0,
                    op0=ADD,
                    op1=MULT,
                )
            nc.scalar.activation(
                out=xc_sb[:, LAST, :],
                in_=xc_sb[:, LAST, :],
                func=IDENTITY,
                bias=neg_mu[:, LAST : LAST + 1],
                scale=1.0,
            )

            gs = work.tile([P, PACK, D], F32)
            sum_gs = stats.tile([P, PACK], F32)
            for j in range(PACK):
                nc.vector.scalar_tensor_tensor(
                    out=gs[:, j, :],
                    in0=grads[n][:, j, :],
                    scalar=rstd_sb[:, n, j : j + 1],
                    in1=gains[n][:],
                    op0=MULT,
                    op1=MULT,
                    accum_out=sum_gs[:, j : j + 1],
                )
            mean_gs = stats.tile([P, PACK], F32)
            nc.vector.tensor_scalar(
                out=mean_gs[:], in0=sum_gs[:], scalar1=1.0 / D, scalar2=None, op0=MULT
            )

            slope = stats.tile([P, PACK], F32)
            for j in range(PACK):
                product = work.tile([P, D], F32)
                nc.vector.scalar_tensor_tensor(
                    out=product[:],
                    in0=xc_sb[:, j, :],
                    scalar=a2_over_d[:, n, j : j + 1],
                    in1=gs[:, j, :],
                    op0=MULT,
                    op1=MULT,
                    accum_out=slope[:, j : j + 1],
                )
                if j < LAST:
                    nc.scalar.activation(
                        out=xc_sb[:, j, :],
                        in_=xc_sb[:, j, :],
                        func=IDENTITY,
                        bias=mean_gs[:, j : j + 1],
                        scale=slope[:, j : j + 1],
                    )
                else:
                    nc.vector.tensor_scalar(
                        out=xc_sb[:, j, :],
                        in0=xc_sb[:, j, :],
                        scalar1=slope[:, j : j + 1],
                        scalar2=mean_gs[:, j : j + 1],
                        op0=MULT,
                        op1=ADD,
                    )

            if n > 0:
                multiply(n - 1, range(EARLY_TILES, TILES))
            if n == 0:
                regroup_proto(0, (nc.scalar.copy, nc.vector.tensor_copy))
            if n + 1 < NQ:
                regroup_proto(n + 1, (nc.scalar.copy, nc.scalar.copy))

            dprc_codes = work.tile([P, D], U32, align_bytes=64)
            dprc_scales = work.tile([P, D], U8, align_bytes=64)
            proto_codes = work.tile([P, W], U32, align_bytes=64)
            proto_scales = work.tile([P, W], U8, align_bytes=64)
            operands[n] = (dprc_codes, dprc_scales, proto_codes, proto_scales)
            pieces = {}

            def subtract(piece):
                cols = slice(piece * D // PIECES, (piece + 1) * D // PIECES)
                dprc_grouped = work.tile([P, D // PIECES, PACK], BF16, bufs=3, align_bytes=64)
                pieces[piece] = dprc_grouped
                nc.vector.tensor_tensor(
                    out=by_column(dprc_grouped[:]),
                    in0=by_row(gs[:, :, cols]),
                    in1=by_row(xc_sb[:, :, cols]),
                    op=SUBTRACT,
                )

            def quantise(piece):
                cols = slice(piece * D // PIECES, (piece + 1) * D // PIECES)
                nc.vector.quantize_mx(
                    out=dprc_codes[:, cols].bitcast(E5M2_X4),
                    scales=dprc_scales[:, cols],
                    in_=pieces[piece][:].rearrange("p d j -> p (d j)"),
                )

            subtract(0)
            nc.vector.quantize_mx(
                out=proto_codes[:].bitcast(E4M3_X4),
                scales=proto_scales[:],
                in_=proto_groups[n][:].rearrange("p w j -> p (w j)"),
            )
            quantise(0)
            subtract(1)
            for piece in range(2, PIECES):
                subtract(piece)
                quantise(piece - 1)
            quantise(PIECES - 1)
            multiply(n, range(EARLY_TILES))
        multiply(NQ - 1, range(EARLY_TILES, TILES))
